import numpy as np
import ml_dtypes


def mxq(x, axis, fmt="e4m3"):
    dtype, down = {"e4m3": (ml_dtypes.float8_e4m3fn, 7), "e5m2": (ml_dtypes.float8_e5m2, 14)}[fmt]
    v = np.moveaxis(np.asarray(x, np.float32).astype(ml_dtypes.bfloat16).astype(np.float64), axis, -1)
    blocks = v.reshape(v.shape[:-1] + (-1, 32))
    amax = np.abs(blocks).max(-1, keepdims=True)
    byte = np.maximum(np.where(amax > 0, np.frexp(amax)[1] - 1 + 127, 0) - down, 1)
    scale = np.exp2(byte - 127.0)
    codes = (blocks / scale).astype(np.float32).astype(dtype).astype(np.float64)
    return np.moveaxis((codes * scale).reshape(v.shape), -1, axis)


WIDE = False


def mx_kscale(k):
    if not WIDE:
        return np.ones(k)
    levels = np.array([10, -10, 5, -5, 0])
    a = np.random.permutation(np.resize(levels, k // 512 * 4)).reshape(k // 512, 4)
    idx = np.arange(k)
    return np.exp2(a[idx // 512, idx % 128 // 32])


BF16 = ml_dtypes.bfloat16


def bf(x):
    return np.asarray(x, np.float32).astype(BF16)


def f64(x):
    return np.asarray(x).astype(np.float64)


E2M1 = np.array([0.0, 0.5, 1.0, 1.5, 2.0, 3.0, 4.0, 6.0, -0.0, -0.5, -1.0, -1.5, -2.0, -3.0, -4.0, -6.0])


def pack_weight(w, fmt):
    k, n = w.shape
    w = f64(bf(w)).reshape(k // 32, 32, n)
    amax = np.abs(w).max(1)
    if fmt == "e4m3":
        byte = np.frexp(amax)[1] - 1 + 127 - 7
    else:
        mant, ex = np.frexp(amax / 6.0)
        byte = np.where(mant > 0.5, ex, ex - 1) + 127
    byte = np.clip(np.where(amax > 0, byte, 1), 1, 254)
    scaled = (w * np.exp2(127.0 - byte)[:, None, :]).reshape(k, n).astype(np.float32)
    by_word = np.ascontiguousarray(scaled.reshape(k // 512, 128, 4, n).transpose(0, 1, 3, 2))
    if fmt == "e4m3":
        words = by_word.astype(ml_dtypes.float8_e4m3fn).view(np.uint8)
    else:
        c = by_word.astype(ml_dtypes.float4_e2m1fn).view(np.uint8) & 0xF
        words = c[..., 0::2] | (c[..., 1::2] << 4)
    return np.ascontiguousarray(words), np.ascontiguousarray(byte.astype(np.uint8).reshape(k // 512, 16, n))


def unpack_weight(words, scales, fmt):
    g, p, n, _ = words.shape
    if fmt == "e4m3":
        vals = np.ascontiguousarray(words).view(ml_dtypes.float8_e4m3fn).astype(np.float64)
    else:
        nib = np.empty((g, p, n, 4), np.uint8)
        nib[..., 0::2] = words & 0xF
        nib[..., 1::2] = words >> 4
        vals = E2M1[nib]
    vals = vals * np.repeat(np.exp2(scales.astype(np.float64) - 127.0), 8, axis=1)[..., None]
    return vals.transpose(0, 1, 3, 2).reshape(g * 512, n)

def pack4(w):
    words, scales = pack_weight(w, "e2m1")
    return words.reshape(words.shape[0], 128, -1), scales


def unpack4(words, scales):
    return unpack_weight(words.reshape(words.shape[0], 128, -1, 2), scales, "e2m1")


B, A, C, P = 64, 11, 1024, 256
N = A * A + 1


def scramble(y):
    return y.transpose(0, 2, 1).reshape(B, N, C)


def unscramble(z):
    return z.reshape(B, C, N).transpose(0, 2, 1)


def setup_inputs():
    s = mx_kscale(C)
    z = np.random.standard_normal((B, N, C)) * 1.6 / np.sqrt(N) * s
    w = np.random.standard_normal((P, C)) * 2.0 / np.sqrt(C) / s
    words, scales = pack4(np.ascontiguousarray(w.T))
    return {"y_attn": bf(np.ascontiguousarray(unscramble(z))),
            "w_proj_words": words,
            "w_proj_scales": scales,
            "b_proj": bf(np.random.standard_normal(P) * 0.1)}


def reference(y_attn, w_proj_words, w_proj_scales, b_proj):
    z = scramble(f64(y_attn))
    return (mxq(z, 2, "e4m3") @ unpack4(w_proj_words, w_proj_scales)) + f64(b_proj)

@@ -1,0 +1,218 @@
+from contextlib import ExitStack
+
+import concourse.mybir as mybir
+from concourse.masks import make_identity
+
+BF16 = mybir.dt.bfloat16
+F32 = mybir.dt.float32
+I32 = mybir.dt.int32
+U32 = mybir.dt.uint32
+U8 = mybir.dt.uint8
+FP8X4 = mybir.dt.float8_e4m3fn_x4
+FP4X4 = mybir.dt.float4_e2m1fn_x4
+
+IMAGES, TOKENS, CHANNELS, FEATURES = 64, 122, 1024, 256
+FLOPS = 2 * IMAGES * TOKENS * CHANNELS * FEATURES
+
+P = 128
+PACK = 4
+K_PASS = P * PACK
+PASSES = CHANNELS // K_PASS
+STRAND_CHANNELS = CHANNELS // 2
+STRAND_ROWS = TOKENS // 2
+N_TILE = 128
+
+CHUNK = 256
+CHUNKS = STRAND_CHANNELS // CHUNK
+CHUNK_PASSES = CHUNK * TOKENS // K_PASS
+DOUBLE_COLUMNS = CHUNK // 2
+PLANE = DOUBLE_COLUMNS * TOKENS
+
+QUADS = 8
+X_BUFS = 4
+VECTOR_COLUMNS = DOUBLE_COLUMNS * 5 // 8
+RUN = 4
+
+ROUND = 4
+OUT_BUFS = 10
+
+
+def token_groups():
+    groups = []
+    for v in range(2):
+        quads = (TOKENS - 2 * v + 2) // 4
+        for first in range(0, quads, QUADS):
+            groups.append((v, first, min(QUADS, quads - first)))
+    return groups
+
+
+def tile_attention_pa_t_kernel(tc, y_attn, w_proj_words, w_proj_scales, b_proj, out):
+    nc = tc.nc
+    out_rows = out.flatten_outer_dims().rearrange("(s r) o -> s r o", r=STRAND_ROWS)
+
+    with ExitStack() as stack:
+        keep = stack.enter_context(tc.tile_pool(name="keep", bufs=1))
+        x_pool = stack.enter_context(tc.tile_pool(name="x", bufs=X_BUFS))
+        work = stack.enter_context(tc.tile_pool(name="work", bufs=2))
+        out_pool = stack.enter_context(tc.tile_pool(name="out", bufs=OUT_BUFS))
+        psum_t = stack.enter_context(tc.psum_pool(name="psum_t", bufs=6))
+        psum_o = stack.enter_context(tc.psum_pool(name="psum_o", bufs=2))
+        stack.enter_context(tc.manual_schedule())
+
+        planes = [
+            keep.tile([P, 2, PLANE], BF16, name="planes%d" % chunk, align_bytes=64)
+            for chunk in range(CHUNKS)
+        ]
+        ident = keep.tile([P, P], F32, name="ident")
+        ones = keep.tile([P, P], BF16, name="ones")
+        bias_rows = keep.tile([P, FEATURES], BF16, name="bias_rows")
+        bias = keep.tile([P, FEATURES], F32, name="bias")
+        w_words = keep.tile([P, PASSES, 2 * FEATURES], U8, name="w_words", align_bytes=64)
+        w_scales = keep.tile([P, PASSES, FEATURES], U8, name="w_scales", align_bytes=64)
+
+        def load_tokens(chunk, v, first, quads):
+            x = x_pool.tile([P, 2 * QUADS, CHUNK], BF16, name="x")
+            for h in range(2):
+                channel = STRAND_CHANNELS * h + CHUNK * chunk
+                for e in range(2):
+                    token = 4 * first + 2 * v + e
+                    nc.sync.dma_start(
+                        out=x[h:P:2, e : 2 * quads : 2, :],
+                        in_=y_attn[:, token : token + 4 * (quads - 1) + 1 : 4, channel : channel + CHUNK],
+                    )
+            return x
+
+        def sort_pairs(x, chunk, v, first, quads):
+            rows = 2 * quads
+            for parity in range(2):
+                plane = (v + parity) % 2
+                start = 2 * first + parity * (60 + 2 * v)
+                dst = planes[chunk][:, plane, :].rearrange("p (c r) -> p c r", r=TOKENS)
+                dst = dst[:, :, start : start + rows]
+                src = x[:, 0:rows, :].rearrange("p r (c two) -> p c r two", two=2)[:, :, :, parity]
+                nc.vector.tensor_copy(
+                    out=dst[:, 0:VECTOR_COLUMNS, :].rearrange("p (q i) r -> p q r i", i=RUN),
+                    in_=src[:, 0:VECTOR_COLUMNS, :].rearrange("p (q i) r -> p q r i", i=RUN),
+                )
+                nc.scalar.copy(
+                    out=dst[:, VECTOR_COLUMNS:, :].rearrange("p (q i) r -> p q r i", i=RUN),
+                    in_=src[:, VECTOR_COLUMNS:, :].rearrange("p (q i) r -> p q r i", i=RUN),
+                )
+
+        def transpose_rows(rows):
+            tiles = []
+            for first in range(0, len(rows), 2):
+                grouped = work.tile([P, 2, PASSES, P, PACK], BF16, name="grouped", bufs=4, align_bytes=64)
+                for r, row in enumerate(rows[first : first + 2]):
+                    turned = psum_t.tile([P, PASSES, 2, P], F32, name="turned")
+                    for g in range(PASSES):
+                        chunk, local = divmod(PASSES * row + g, CHUNK_PASSES)
+                        for half in range(2):
+                            pairs = planes[chunk][:, half, :].bitcast(F32)
+                            nc.tensor.transpose(
+                                out=turned[:, g, half, :],
+                                in_=pairs[:, P * local : P * (local + 1)],
+                                identity=ident[:],
+                            )
+                    nc.scalar.copy(
+                        out=grouped[:, r].bitcast(F32),
+                        in_=turned[:].rearrange("p g half s -> p g s half"),
+                    )
+                tiles.append(grouped)
+            return tiles
+
+        def quantise_rows(rows, tiles):
+            codes = work.tile([P, ROUND, PASSES, P], U32, name="codes", align_bytes=64)
+            scales = work.tile([P, ROUND, PASSES, P], U8, name="scales", align_bytes=64)
+            for t, grouped in enumerate(tiles):
+                count = len(rows[2 * t : 2 * t + 2])
+                nc.vector.quantize_mx(
+                    out=codes[:, 2 * t : 2 * t + count].rearrange("p r g s -> p (r g s)").bitcast(FP8X4),
+                    scales=scales[:, 2 * t : 2 * t + count].rearrange("p r g s -> p (r g s)"),
+                    in_=grouped[:, 0:count].rearrange("p r g s t -> p (r g s t)"),
+                )
+            return codes, scales
+
+        def multiply_rows(rows, codes, scales):
+            banks = []
+            for first in range(0, len(rows), 2):
+                acc = psum_o.tile([P, 2, FEATURES], F32, name="acc")
+                for r in range(len(rows[first : first + 2])):
+                    for n in range(0, FEATURES, N_TILE):
+                        for g in range(PASSES):
+                            nc.tensor.matmul_mx(
+                                out=acc[:, r, n : n + N_TILE],
+                                lhsT=codes[:, first + r, g, :].bitcast(FP8X4),
+                                lhsT_scale=scales[:, first + r, g, :],
+                                rhs=w_words[:, g, 2 * n : 2 * (n + N_TILE)].bitcast(FP4X4),
+                                rhs_scale=w_scales[:, g, n : n + N_TILE],
+                                start=(g == 0),
+                                stop=(g == PASSES - 1),
+                            )
+                banks.append(acc)
+            return banks
+
+        def add_bias(rows, banks):
+            result = out_pool.tile([P, ROUND, FEATURES], F32, name="result")
+            for t, acc in enumerate(banks):
+                count = len(rows[2 * t : 2 * t + 2])
+                nc.vector.tensor_tensor(
+                    out=result[:, 2 * t : 2 * t + count, :],
+                    in0=acc[:, 0:count, :],
+                    in1=bias[:].unsqueeze(1).to_broadcast([P, count, FEATURES]),
+                    op=mybir.AluOpType.add,
+                )
+            return result
+
+        def store_rows(rows, result):
+            nc.sync.dma_start(out=out_rows[:, rows[0] : rows[0] + len(rows), :], in_=result[:, 0 : len(rows), :])
+
+        make_identity(nc, ident[:])
+        nc.vector.memset(ones[:], 1.0)
+        nc.vector.memset(bias_rows[:], 0.0)
+        nc.vector.memset(w_scales[:].bitcast(I32), 0)
+
+        tiles_to_load = [(chunk,) + group for chunk in range(CHUNKS) for group in token_groups()]
+        loaded = [load_tokens(*tiles_to_load[t]) for t in range(2)]
+
+        nc.sync.dma_start(out=w_words[:].bitcast(I32), in_=w_proj_words.rearrange("g p n -> p g n").bitcast(I32))
+        for quadrant in range(4):
+            nc.sync.dma_start(
+                out=w_scales[32 * quadrant : 32 * quadrant + 4].bitcast(I32),
+                in_=w_proj_scales[:, 4 * quadrant : 4 * quadrant + 4, :].rearrange("g r n -> r g n").bitcast(I32),
+            )
+        nc.sync.dma_start(out=bias_rows[0:1, :], in_=b_proj.rearrange("(o n) -> o n", o=1))
+        loaded += [load_tokens(*tiles_to_load[t]) for t in range(2, X_BUFS)]
+
+        rounds = [list(range(r, min(r + ROUND, STRAND_ROWS))) for r in range(0, STRAND_ROWS, ROUND)]
+        early_rounds = CHUNK_PASSES // (PASSES * ROUND)
+        state = {}
+
+        def start_round(k):
+            state[k] = quantise_rows(rounds[k], transpose_rows(rounds[k]))
+
+        def step(k):
+            tiles = transpose_rows(rounds[k + 1]) if k + 1 < len(rounds) else None
+            banks = multiply_rows(rounds[k], *state[k])
+            if tiles is not None:
+                state[k + 1] = quantise_rows(rounds[k + 1], tiles)
+            return add_bias(rounds[k], banks)
+
+        per_chunk = len(tiles_to_load) // CHUNKS
+        waiting = []
+        for t, (chunk, v, first, quads) in enumerate(tiles_to_load):
+            sort_pairs(loaded[t], chunk, v, first, quads)
+            if t + X_BUFS < len(tiles_to_load):
+                loaded.append(load_tokens(*tiles_to_load[t + X_BUFS]))
+            if t == per_chunk - 1:
+                spread = psum_o.tile([P, 2, FEATURES], F32, name="acc")
+                nc.tensor.matmul(out=spread[:, 0, :], lhsT=ones[:], rhs=bias_rows[:], start=True, stop=True)
+                nc.vector.tensor_copy(out=bias[:], in_=spread[:, 0, :])
+                start_round(0)
+            k = t - per_chunk
+            if 0 <= k < early_rounds - 1:
+                waiting.append((rounds[k], step(k)))
+        for rows, result in waiting:
+            store_rows(rows, result)
+        for k in range(early_rounds - 1, len(rounds)):
+            store_rows(rounds[k], step(k))

@@ -184,35 +184,49 @@ def tile_attention_pa_t_kernel(tc, y_attn, w_proj_words, w_proj_scales, b_proj, 
         nc.sync.dma_start(out=bias_rows[0:1, :], in_=b_proj.rearrange("(o n) -> o n", o=1))
         loaded += [load_tokens(*tiles_to_load[t]) for t in range(2, X_BUFS)]
 
-        rounds = [list(range(r, min(r + ROUND, STRAND_ROWS))) for r in range(0, STRAND_ROWS, ROUND)]
-        early_rounds = CHUNK_PASSES // (PASSES * ROUND)
-        state = {}
+        def rounds_of(chunk):
+            first_row = CHUNK_PASSES * chunk // PASSES
+            end_row = CHUNK_PASSES * (chunk + 1) // PASSES
+            return [list(range(r, min(r + ROUND, end_row))) for r in range(first_row, end_row, ROUND)]
 
-        def start_round(k):
-            state[k] = quantise_rows(rounds[k], transpose_rows(rounds[k]))
+        def first_round(rounds):
+            return quantise_rows(rounds[0], transpose_rows(rounds[0]))
 
-        def step(k):
-            tiles = transpose_rows(rounds[k + 1]) if k + 1 < len(rounds) else None
-            banks = multiply_rows(rounds[k], *state[k])
-            if tiles is not None:
-                state[k + 1] = quantise_rows(rounds[k + 1], tiles)
-            return add_bias(rounds[k], banks)
+        def step(rounds, k, ready):
+            following = None
+            if k + 1 < len(rounds):
+                tiles = transpose_rows(rounds[k + 1])
+            banks = multiply_rows(rounds[k], *ready)
+            if k + 1 < len(rounds):
+                following = quantise_rows(rounds[k + 1], tiles)
+            return add_bias(rounds[k], banks), following
 
-        per_chunk = len(tiles_to_load) // CHUNKS
-        waiting = []
-        for t, (chunk, v, first, quads) in enumerate(tiles_to_load):
-            sort_pairs(loaded[t], chunk, v, first, quads)
+        def sort_and_load_ahead(t):
+            sort_pairs(loaded[t], *tiles_to_load[t])
             if t + X_BUFS < len(tiles_to_load):
                 loaded.append(load_tokens(*tiles_to_load[t + X_BUFS]))
-            if t == per_chunk - 1:
-                spread = psum_o.tile([P, 2, FEATURES], F32, name="acc")
-                nc.tensor.matmul(out=spread[:, 0, :], lhsT=ones[:], rhs=bias_rows[:], start=True, stop=True)
-                nc.vector.tensor_copy(out=bias[:], in_=spread[:, 0, :])
-                start_round(0)
-            k = t - per_chunk
-            if 0 <= k < early_rounds - 1:
-                waiting.append((rounds[k], step(k)))
-        for rows, result in waiting:
+
+        per_chunk = len(tiles_to_load) // CHUNKS
+        for t in range(per_chunk):
+            sort_and_load_ahead(t)
+
+        spread = psum_o.tile([P, 2, FEATURES], F32, name="acc")
+        nc.tensor.matmul(out=spread[:, 0, :], lhsT=ones[:], rhs=bias_rows[:], start=True, stop=True)
+        nc.vector.tensor_copy(out=bias[:], in_=spread[:, 0, :])
+
+        early = rounds_of(0)
+        assert len(early) == per_chunk
+        ready = first_round(early)
+        results = []
+        for k in range(len(early)):
+            result, ready = step(early, k, ready)
+            results.append(result)
+            sort_and_load_ahead(per_chunk + k)
+        for rows, result in zip(early, results):
             store_rows(rows, result)
-        for k in range(early_rounds - 1, len(rounds)):
-            store_rows(rounds[k], step(k))
+
+        late = rounds_of(1)
+        ready = first_round(late)
+        for k in range(len(late)):
+            result, ready = step(late, k, ready)
+            store_rows(late[k], result)

@@ -22,19 +22,22 @@ STRAND_CHANNELS = CHANNELS // 2
 STRAND_ROWS = TOKENS // 2
 N_TILE = 128
 
-CHUNK = 256
-CHUNKS = STRAND_CHANNELS // CHUNK
-CHUNK_PASSES = CHUNK * TOKENS // K_PASS
-DOUBLE_COLUMNS = CHUNK // 2
-PLANE = DOUBLE_COLUMNS * TOKENS
+UNITS = (128, 128, 128, 128)
+assert sum(UNITS) == STRAND_CHANNELS
+WORDS_IN_DOUBLE_COLUMN = TOKENS // 2
+PLANE = STRAND_CHANNELS // 2 * TOKENS
 
-QUADS = 8
+QUADS = 16
 X_BUFS = 4
-VECTOR_COLUMNS = DOUBLE_COLUMNS * 5 // 8
 RUN = 4
 
 ROUND = 4
-OUT_BUFS = 10
+OUT_BUFS = 4
+LEAD = 0
+
+
+def vector_columns(columns):
+    return columns * 5 // 8 // 8 * 8
 
 
 def token_groups():
@@ -59,10 +62,7 @@ def tile_attention_pa_t_kernel(tc, y_attn, w_proj_words, w_proj_scales, b_proj, 
         psum_o = stack.enter_context(tc.psum_pool(name="psum_o", bufs=2))
         stack.enter_context(tc.manual_schedule())
 
-        planes = [
-            keep.tile([P, 2, PLANE], BF16, name="planes%d" % chunk, align_bytes=64)
-            for chunk in range(CHUNKS)
-        ]
+        planes = keep.tile([P, 2, PLANE], BF16, name="planes", align_bytes=64)
         ident = keep.tile([P, P], F32, name="ident")
         ones = keep.tile([P, P], BF16, name="ones")
         bias_rows = keep.tile([P, FEATURES], BF16, name="bias_rows")
@@ -70,33 +70,37 @@ def tile_attention_pa_t_kernel(tc, y_attn, w_proj_words, w_proj_scales, b_proj, 
         w_words = keep.tile([P, PASSES, 2 * FEATURES], U8, name="w_words", align_bytes=64)
         w_scales = keep.tile([P, PASSES, FEATURES], U8, name="w_scales", align_bytes=64)
 
-        def load_tokens(chunk, v, first, quads):
-            x = x_pool.tile([P, 2 * QUADS, CHUNK], BF16, name="x")
+        def load_tokens(unit, v, first, quads):
+            width = UNITS[unit]
+            x = x_pool.tile([P, 2 * QUADS, width], BF16, name="x")
             for h in range(2):
-                channel = STRAND_CHANNELS * h + CHUNK * chunk
+                channel = STRAND_CHANNELS * h + sum(UNITS[:unit])
                 for e in range(2):
                     token = 4 * first + 2 * v + e
                     nc.sync.dma_start(
                         out=x[h:P:2, e : 2 * quads : 2, :],
-                        in_=y_attn[:, token : token + 4 * (quads - 1) + 1 : 4, channel : channel + CHUNK],
+                        in_=y_attn[:, token : token + 4 * (quads - 1) + 1 : 4, channel : channel + width],
                     )
             return x
 
-        def sort_pairs(x, chunk, v, first, quads):
+        def sort_pairs(x, unit, v, first, quads):
             rows = 2 * quads
+            column = sum(UNITS[:unit]) // 2
+            columns = UNITS[unit] // 2
+            share = vector_columns(columns)
             for parity in range(2):
                 plane = (v + parity) % 2
                 start = 2 * first + parity * (60 + 2 * v)
-                dst = planes[chunk][:, plane, :].rearrange("p (c r) -> p c r", r=TOKENS)
-                dst = dst[:, :, start : start + rows]
+                dst = planes[:, plane, :].rearrange("p (c r) -> p c r", r=TOKENS)
+                dst = dst[:, column : column + columns, start : start + rows]
                 src = x[:, 0:rows, :].rearrange("p r (c two) -> p c r two", two=2)[:, :, :, parity]
                 nc.vector.tensor_copy(
-                    out=dst[:, 0:VECTOR_COLUMNS, :].rearrange("p (q i) r -> p q r i", i=RUN),
-                    in_=src[:, 0:VECTOR_COLUMNS, :].rearrange("p (q i) r -> p q r i", i=RUN),
+                    out=dst[:, 0:share, :].rearrange("p (q i) r -> p q r i", i=RUN),
+                    in_=src[:, 0:share, :].rearrange("p (q i) r -> p q r i", i=RUN),
                 )
                 nc.scalar.copy(
-                    out=dst[:, VECTOR_COLUMNS:, :].rearrange("p (q i) r -> p q r i", i=RUN),
-                    in_=src[:, VECTOR_COLUMNS:, :].rearrange("p (q i) r -> p q r i", i=RUN),
+                    out=dst[:, share:, :].rearrange("p (q i) r -> p q r i", i=RUN),
+                    in_=src[:, share:, :].rearrange("p (q i) r -> p q r i", i=RUN),
                 )
 
         def transpose_rows(rows):
@@ -106,12 +110,12 @@ def tile_attention_pa_t_kernel(tc, y_attn, w_proj_words, w_proj_scales, b_proj, 
                 for r, row in enumerate(rows[first : first + 2]):
                     turned = psum_t.tile([P, PASSES, 2, P], F32, name="turned")
                     for g in range(PASSES):
-                        chunk, local = divmod(PASSES * row + g, CHUNK_PASSES)
+                        number = PASSES * row + g
                         for half in range(2):
-                            pairs = planes[chunk][:, half, :].bitcast(F32)
+                            pairs = planes[:, half, :].bitcast(F32)
                             nc.tensor.transpose(
                                 out=turned[:, g, half, :],
-                                in_=pairs[:, P * local : P * (local + 1)],
+                                in_=pairs[:, P * number : P * (number + 1)],
                                 identity=ident[:],
                             )
                     nc.scalar.copy(
@@ -152,7 +156,7 @@ def tile_attention_pa_t_kernel(tc, y_attn, w_proj_words, w_proj_scales, b_proj, 
                 banks.append(acc)
             return banks
 
-        def add_bias(rows, banks):
+        def add_bias_and_store(rows, banks):
             result = out_pool.tile([P, ROUND, FEATURES], F32, name="result")
             for t, acc in enumerate(banks):
                 count = len(rows[2 * t : 2 * t + 2])
@@ -162,9 +166,6 @@ def tile_attention_pa_t_kernel(tc, y_attn, w_proj_words, w_proj_scales, b_proj, 
                     in1=bias[:].unsqueeze(1).to_broadcast([P, count, FEATURES]),
                     op=mybir.AluOpType.add,
                 )
-            return result
-
-        def store_rows(rows, result):
             nc.sync.dma_start(out=out_rows[:, rows[0] : rows[0] + len(rows), :], in_=result[:, 0 : len(rows), :])
 
         make_identity(nc, ident[:])
@@ -172,7 +173,8 @@ def tile_attention_pa_t_kernel(tc, y_attn, w_proj_words, w_proj_scales, b_proj, 
         nc.vector.memset(bias_rows[:], 0.0)
         nc.vector.memset(w_scales[:].bitcast(I32), 0)
 
-        tiles_to_load = [(chunk,) + group for chunk in range(CHUNKS) for group in token_groups()]
+        tiles_to_load = [(unit,) + group for unit in range(len(UNITS)) for group in token_groups()]
+        per_unit = len(token_groups())
         loaded = [load_tokens(*tiles_to_load[t]) for t in range(2)]
 
         nc.sync.dma_start(out=w_words[:].bitcast(I32), in_=w_proj_words.rearrange("g p n -> p g n").bitcast(I32))
@@ -184,49 +186,47 @@ def tile_attention_pa_t_kernel(tc, y_attn, w_proj_words, w_proj_scales, b_proj, 
         nc.sync.dma_start(out=bias_rows[0:1, :], in_=b_proj.rearrange("(o n) -> o n", o=1))
         loaded += [load_tokens(*tiles_to_load[t]) for t in range(2, X_BUFS)]
 
-        def rounds_of(chunk):
-            first_row = CHUNK_PASSES * chunk // PASSES
-            end_row = CHUNK_PASSES * (chunk + 1) // PASSES
-            return [list(range(r, min(r + ROUND, end_row))) for r in range(first_row, end_row, ROUND)]
+        rounds = []
+        first_row = 0
+        for unit in range(len(UNITS)):
+            end_row = sum(UNITS[: unit + 1]) // 2 * WORDS_IN_DOUBLE_COLUMN // (PASSES * P)
+            for r in range(first_row, end_row, ROUND):
+                rounds.append((list(range(r, min(r + ROUND, end_row))), per_unit * (unit + 1)))
+            first_row = end_row
 
-        def first_round(rounds):
-            return quantise_rows(rounds[0], transpose_rows(rounds[0]))
+        state = {"sorted": 0}
 
-        def step(rounds, k, ready):
-            following = None
-            if k + 1 < len(rounds):
-                tiles = transpose_rows(rounds[k + 1])
-            banks = multiply_rows(rounds[k], *ready)
-            if k + 1 < len(rounds):
-                following = quantise_rows(rounds[k + 1], tiles)
-            return add_bias(rounds[k], banks), following
+        def sort_next():
+            t = state["sorted"]
+            if t < len(tiles_to_load):
+                sort_pairs(loaded[t], *tiles_to_load[t])
+                if t + X_BUFS < len(tiles_to_load):
+                    loaded.append(load_tokens(*tiles_to_load[t + X_BUFS]))
+                state["sorted"] = t + 1
 
-        def sort_and_load_ahead(t):
-            sort_pairs(loaded[t], *tiles_to_load[t])
-            if t + X_BUFS < len(tiles_to_load):
-                loaded.append(load_tokens(*tiles_to_load[t + X_BUFS]))
-
-        per_chunk = len(tiles_to_load) // CHUNKS
-        for t in range(per_chunk):
-            sort_and_load_ahead(t)
+        while state["sorted"] < rounds[0][1] + LEAD:
+            sort_next()
 
         spread = psum_o.tile([P, 2, FEATURES], F32, name="acc")
         nc.tensor.matmul(out=spread[:, 0, :], lhsT=ones[:], rhs=bias_rows[:], start=True, stop=True)
         nc.vector.tensor_copy(out=bias[:], in_=spread[:, 0, :])
 
-        early = rounds_of(0)
-        assert len(early) == per_chunk
-        ready = first_round(early)
-        results = []
-        for k in range(len(early)):
-            result, ready = step(early, k, ready)
-            results.append(result)
-            sort_and_load_ahead(per_chunk + k)
-        for rows, result in zip(early, results):
-            store_rows(rows, result)
-
-        late = rounds_of(1)
-        ready = first_round(late)
-        for k in range(len(late)):
-            result, ready = step(late, k, ready)
-            store_rows(late[k], result)
+        ready = quantise_rows(rounds[0][0], transpose_rows(rounds[0][0]))
+        for k in range(len(rounds)):
+            rows = rounds[k][0]
+            following = rounds[k + 1] if k + 1 < len(rounds) else None
+            fresh = following is not None and following[1] > state["sorted"]
+            if fresh:
+                banks = multiply_rows(rows, *ready)
+                while state["sorted"] < following[1]:
+                    sort_next()
+                add_bias_and_store(rows, banks)
+                ready = quantise_rows(following[0], transpose_rows(following[0]))
+            else:
+                if following is not None:
+                    tiles = transpose_rows(following[0])
+                banks = multiply_rows(rows, *ready)
+                sort_next()
+                if following is not None:
+                    ready = quantise_rows(following[0], tiles)
+                add_bias_and_store(rows, banks)

@@ -22,12 +22,12 @@ STRAND_CHANNELS = CHANNELS // 2
 STRAND_ROWS = TOKENS // 2
 N_TILE = 128
 
-UNITS = (128, 128, 128, 128)
+UNITS = (256, 256)
 assert sum(UNITS) == STRAND_CHANNELS
 WORDS_IN_DOUBLE_COLUMN = TOKENS // 2
 PLANE = STRAND_CHANNELS // 2 * TOKENS
 
-QUADS = 16
+QUADS = 8
 X_BUFS = 4
 RUN = 4
 

@@ -32,7 +32,7 @@ X_BUFS = 4
 RUN = 4
 
 ROUND = 4
-OUT_BUFS = 4
+OUT_BUFS = 10
 LEAD = 0
 
 
@@ -166,7 +166,14 @@ def tile_attention_pa_t_kernel(tc, y_attn, w_proj_words, w_proj_scales, b_proj, 
                     in1=bias[:].unsqueeze(1).to_broadcast([P, count, FEATURES]),
                     op=mybir.AluOpType.add,
                 )
-            nc.sync.dma_start(out=out_rows[:, rows[0] : rows[0] + len(rows), :], in_=result[:, 0 : len(rows), :])
+            waiting.append((rows, result))
+            if state["sorted"] + X_BUFS >= len(tiles_to_load):
+                for stored_rows, stored in waiting:
+                    nc.sync.dma_start(
+                        out=out_rows[:, stored_rows[0] : stored_rows[0] + len(stored_rows), :],
+                        in_=stored[:, 0 : len(stored_rows), :],
+                    )
+                waiting.clear()
 
         make_identity(nc, ident[:])
         nc.vector.memset(ones[:], 1.0)
@@ -195,6 +202,7 @@ def tile_attention_pa_t_kernel(tc, y_attn, w_proj_words, w_proj_scales, b_proj, 
             first_row = end_row
 
         state = {"sorted": 0}
+        waiting = []
 
         def sort_next():
             t = state["sorted"]

@@ -27,6 +27,9 @@ assert sum(UNITS) == STRAND_CHANNELS
 WORDS_IN_DOUBLE_COLUMN = TOKENS // 2
 PLANE = STRAND_CHANNELS // 2 * TOKENS
 
+UNIT_PASSES = UNITS[0] * TOKENS // K_PASS
+assert all(width * TOKENS == UNIT_PASSES * K_PASS for width in UNITS)
+
 QUADS = 8
 X_BUFS = 4
 RUN = 4
@@ -62,7 +65,10 @@ def tile_attention_pa_t_kernel(tc, y_attn, w_proj_words, w_proj_scales, b_proj, 
         psum_o = stack.enter_context(tc.psum_pool(name="psum_o", bufs=2))
         stack.enter_context(tc.manual_schedule())
 
-        planes = keep.tile([P, 2, PLANE], BF16, name="planes", align_bytes=64)
+        planes = [
+            keep.tile([P, 2, PLANE // len(UNITS)], BF16, name="planes%d" % unit, align_bytes=64)
+            for unit in range(len(UNITS))
+        ]
         ident = keep.tile([P, P], F32, name="ident")
         ones = keep.tile([P, P], BF16, name="ones")
         bias_rows = keep.tile([P, FEATURES], BF16, name="bias_rows")
@@ -85,14 +91,13 @@ def tile_attention_pa_t_kernel(tc, y_attn, w_proj_words, w_proj_scales, b_proj, 
 
         def sort_pairs(x, unit, v, first, quads):
             rows = 2 * quads
-            column = sum(UNITS[:unit]) // 2
             columns = UNITS[unit] // 2
             share = vector_columns(columns)
             for parity in range(2):
                 plane = (v + parity) % 2
                 start = 2 * first + parity * (60 + 2 * v)
-                dst = planes[:, plane, :].rearrange("p (c r) -> p c r", r=TOKENS)
-                dst = dst[:, column : column + columns, start : start + rows]
+                dst = planes[unit][:, plane, :].rearrange("p (c r) -> p c r", r=TOKENS)
+                dst = dst[:, :, start : start + rows]
                 src = x[:, 0:rows, :].rearrange("p r (c two) -> p c r two", two=2)[:, :, :, parity]
                 nc.vector.tensor_copy(
                     out=dst[:, 0:share, :].rearrange("p (q i) r -> p q r i", i=RUN),
@@ -110,9 +115,9 @@ def tile_attention_pa_t_kernel(tc, y_attn, w_proj_words, w_proj_scales, b_proj, 
                 for r, row in enumerate(rows[first : first + 2]):
                     turned = psum_t.tile([P, PASSES, 2, P], F32, name="turned")
                     for g in range(PASSES):
-                        number = PASSES * row + g
+                        unit, number = divmod(PASSES * row + g, UNIT_PASSES)
                         for half in range(2):
-                            pairs = planes[:, half, :].bitcast(F32)
+                            pairs = planes[unit][:, half, :].bitcast(F32)
                             nc.tensor.transpose(
                                 out=turned[:, g, half, :],
                                 in_=pairs[:, P * number : P * (number + 1)],

@@ -30,12 +30,12 @@ PLANE = STRAND_CHANNELS // 2 * TOKENS
 UNIT_PASSES = UNITS[0] * TOKENS // K_PASS
 assert all(width * TOKENS == UNIT_PASSES * K_PASS for width in UNITS)
 
-QUADS = 8
-X_BUFS = 4
+QUADS = 16
+X_BUFS = 3
 RUN = 4
 
 ROUND = 4
-OUT_BUFS = 10
+OUT_BUFS = 6
 LEAD = 0
 
 
@@ -89,24 +89,23 @@ def tile_attention_pa_t_kernel(tc, y_attn, w_proj_words, w_proj_scales, b_proj, 
                     )
             return x
 
-        def sort_pairs(x, unit, v, first, quads):
+        def sort_pairs(x, unit, v, first, quads, parity):
             rows = 2 * quads
             columns = UNITS[unit] // 2
             share = vector_columns(columns)
-            for parity in range(2):
-                plane = (v + parity) % 2
-                start = 2 * first + parity * (60 + 2 * v)
-                dst = planes[unit][:, plane, :].rearrange("p (c r) -> p c r", r=TOKENS)
-                dst = dst[:, :, start : start + rows]
-                src = x[:, 0:rows, :].rearrange("p r (c two) -> p c r two", two=2)[:, :, :, parity]
-                nc.vector.tensor_copy(
-                    out=dst[:, 0:share, :].rearrange("p (q i) r -> p q r i", i=RUN),
-                    in_=src[:, 0:share, :].rearrange("p (q i) r -> p q r i", i=RUN),
-                )
-                nc.scalar.copy(
-                    out=dst[:, share:, :].rearrange("p (q i) r -> p q r i", i=RUN),
-                    in_=src[:, share:, :].rearrange("p (q i) r -> p q r i", i=RUN),
-                )
+            plane = (v + parity) % 2
+            start = 2 * first + parity * (60 + 2 * v)
+            dst = planes[unit][:, plane, :].rearrange("p (c r) -> p c r", r=TOKENS)
+            dst = dst[:, :, start : start + rows]
+            src = x[:, 0:rows, :].rearrange("p r (c two) -> p c r two", two=2)[:, :, :, parity]
+            nc.vector.tensor_copy(
+                out=dst[:, 0:share, :].rearrange("p (q i) r -> p q r i", i=RUN),
+                in_=src[:, 0:share, :].rearrange("p (q i) r -> p q r i", i=RUN),
+            )
+            nc.scalar.copy(
+                out=dst[:, share:, :].rearrange("p (q i) r -> p q r i", i=RUN),
+                in_=src[:, share:, :].rearrange("p (q i) r -> p q r i", i=RUN),
+            )
 
         def transpose_rows(rows):
             tiles = []
@@ -172,7 +171,7 @@ def tile_attention_pa_t_kernel(tc, y_attn, w_proj_words, w_proj_scales, b_proj, 
                     op=mybir.AluOpType.add,
                 )
             waiting.append((rows, result))
-            if state["sorted"] + X_BUFS >= len(tiles_to_load):
+            if state["sorted"] // 2 + X_BUFS >= len(tiles_to_load):
                 for stored_rows, stored in waiting:
                     nc.sync.dma_start(
                         out=out_rows[:, stored_rows[0] : stored_rows[0] + len(stored_rows), :],
@@ -203,19 +202,23 @@ def tile_attention_pa_t_kernel(tc, y_attn, w_proj_words, w_proj_scales, b_proj, 
         for unit in range(len(UNITS)):
             end_row = sum(UNITS[: unit + 1]) // 2 * WORDS_IN_DOUBLE_COLUMN // (PASSES * P)
             for r in range(first_row, end_row, ROUND):
-                rounds.append((list(range(r, min(r + ROUND, end_row))), per_unit * (unit + 1)))
+                rounds.append((list(range(r, min(r + ROUND, end_row))), 2 * per_unit * (unit + 1)))
             first_row = end_row
+
+        last_rows, last_need = rounds.pop()
+        rounds.append((last_rows[:2], last_need))
+        rounds.append((last_rows[2:], last_need))
 
         state = {"sorted": 0}
         waiting = []
 
         def sort_next():
-            t = state["sorted"]
+            t, parity = divmod(state["sorted"], 2)
             if t < len(tiles_to_load):
-                sort_pairs(loaded[t], *tiles_to_load[t])
-                if t + X_BUFS < len(tiles_to_load):
+                sort_pairs(loaded[t], *tiles_to_load[t], parity)
+                if parity == 1 and t + X_BUFS < len(tiles_to_load):
                     loaded.append(load_tokens(*tiles_to_load[t + X_BUFS]))
-                state["sorted"] = t + 1
+                state["sorted"] += 1
 
         while state["sorted"] < rounds[0][1] + LEAD:
             sort_next()
@@ -239,7 +242,8 @@ def tile_attention_pa_t_kernel(tc, y_attn, w_proj_words, w_proj_scales, b_proj, 
                 if following is not None:
                     tiles = transpose_rows(following[0])
                 banks = multiply_rows(rows, *ready)
-                sort_next()
+                for half_sort in range(1):
+                    sort_next()
                 if following is not None:
                     ready = quantise_rows(following[0], tiles)
                 add_bias_and_store(rows, banks)

@@ -186,16 +186,16 @@ def tile_attention_pa_t_kernel(tc, y_attn, w_proj_words, w_proj_scales, b_proj, 
 
         tiles_to_load = [(unit,) + group for unit in range(len(UNITS)) for group in token_groups()]
         per_unit = len(token_groups())
-        loaded = [load_tokens(*tiles_to_load[t]) for t in range(2)]
+        loaded = [load_tokens(*tiles_to_load[t]) for t in range(X_BUFS)]
 
-        nc.sync.dma_start(out=w_words[:].bitcast(I32), in_=w_proj_words.rearrange("g p n -> p g n").bitcast(I32))
-        for quadrant in range(4):
-            nc.sync.dma_start(
-                out=w_scales[32 * quadrant : 32 * quadrant + 4].bitcast(I32),
-                in_=w_proj_scales[:, 4 * quadrant : 4 * quadrant + 4, :].rearrange("g r n -> r g n").bitcast(I32),
-            )
-        nc.sync.dma_start(out=bias_rows[0:1, :], in_=b_proj.rearrange("(o n) -> o n", o=1))
-        loaded += [load_tokens(*tiles_to_load[t]) for t in range(2, X_BUFS)]
+        def load_weights():
+            nc.sync.dma_start(out=w_words[:].bitcast(I32), in_=w_proj_words.rearrange("g p n -> p g n").bitcast(I32))
+            for quadrant in range(4):
+                nc.sync.dma_start(
+                    out=w_scales[32 * quadrant : 32 * quadrant + 4].bitcast(I32),
+                    in_=w_proj_scales[:, 4 * quadrant : 4 * quadrant + 4, :].rearrange("g r n -> r g n").bitcast(I32),
+                )
+            nc.sync.dma_start(out=bias_rows[0:1, :], in_=b_proj.rearrange("(o n) -> o n", o=1))
 
         rounds = []
         first_row = 0
@@ -217,6 +217,8 @@ def tile_attention_pa_t_kernel(tc, y_attn, w_proj_words, w_proj_scales, b_proj, 
             if t < len(tiles_to_load):
                 sort_pairs(loaded[t], *tiles_to_load[t], parity)
                 if parity == 1 and t + X_BUFS < len(tiles_to_load):
+                    if t + X_BUFS == per_unit:
+                        load_weights()
                     loaded.append(load_tokens(*tiles_to_load[t + X_BUFS]))
                 state["sorted"] += 1
 

@@ -31,6 +31,7 @@ UNIT_PASSES = UNITS[0] * TOKENS // K_PASS
 assert all(width * TOKENS == UNIT_PASSES * K_PASS for width in UNITS)
 
 QUADS = 16
+GROUPS = (((8, 8, 15), (16, 8, 6)), ((16, 15), (16, 14)))
 X_BUFS = 3
 RUN = 4
 
@@ -43,12 +44,14 @@ def vector_columns(columns):
     return columns * 5 // 8 // 8 * 8
 
 
-def token_groups():
+def token_groups(unit):
     groups = []
     for v in range(2):
-        quads = (TOKENS - 2 * v + 2) // 4
-        for first in range(0, quads, QUADS):
-            groups.append((v, first, min(QUADS, quads - first)))
+        first = 0
+        for quads in GROUPS[unit][v]:
+            groups.append((v, first, quads))
+            first += quads
+        assert first == (TOKENS - 2 * v + 2) // 4
     return groups
 
 
@@ -184,8 +187,7 @@ def tile_attention_pa_t_kernel(tc, y_attn, w_proj_words, w_proj_scales, b_proj, 
         nc.vector.memset(bias_rows[:], 0.0)
         nc.vector.memset(w_scales[:].bitcast(I32), 0)
 
-        tiles_to_load = [(unit,) + group for unit in range(len(UNITS)) for group in token_groups()]
-        per_unit = len(token_groups())
+        tiles_to_load = [(unit,) + group for unit in range(len(UNITS)) for group in token_groups(unit)]
         loaded = [load_tokens(*tiles_to_load[t]) for t in range(X_BUFS)]
 
         def load_weights():
@@ -202,7 +204,7 @@ def tile_attention_pa_t_kernel(tc, y_attn, w_proj_words, w_proj_scales, b_proj, 
         for unit in range(len(UNITS)):
             end_row = sum(UNITS[: unit + 1]) // 2 * WORDS_IN_DOUBLE_COLUMN // (PASSES * P)
             for r in range(first_row, end_row, ROUND):
-                rounds.append((list(range(r, min(r + ROUND, end_row))), 2 * per_unit * (unit + 1)))
+                rounds.append((list(range(r, min(r + ROUND, end_row))), 2 * sum(len(token_groups(u)) for u in range(unit + 1))))
             first_row = end_row
 
         last_rows, last_need = rounds.pop()
@@ -217,7 +219,7 @@ def tile_attention_pa_t_kernel(tc, y_attn, w_proj_words, w_proj_scales, b_proj, 
             if t < len(tiles_to_load):
                 sort_pairs(loaded[t], *tiles_to_load[t], parity)
                 if parity == 1 and t + X_BUFS < len(tiles_to_load):
-                    if t + X_BUFS == per_unit:
+                    if t + X_BUFS == len(token_groups(0)):
                         load_weights()
                     loaded.append(load_tokens(*tiles_to_load[t + X_BUFS]))
                 state["sorted"] += 1

@@ -24,35 +24,24 @@ N_TILE = 128
 
 UNITS = (256, 256)
 assert sum(UNITS) == STRAND_CHANNELS
-WORDS_IN_DOUBLE_COLUMN = TOKENS // 2
+UNIT_CHANNELS = UNITS[0]
+UNIT_COLUMNS = UNIT_CHANNELS // 2
 PLANE = STRAND_CHANNELS // 2 * TOKENS
+UNIT_PASSES = UNIT_CHANNELS * TOKENS // K_PASS
+assert UNIT_CHANNELS * TOKENS == UNIT_PASSES * K_PASS
 
-UNIT_PASSES = UNITS[0] * TOKENS // K_PASS
-assert all(width * TOKENS == UNIT_PASSES * K_PASS for width in UNITS)
-
-QUADS = 16
-GROUPS = (((8, 8, 15), (16, 8, 6)), ((16, 15), (16, 14)))
-X_BUFS = 3
+X_ROW = (0, 62)
+LOADS = (
+    ((0, 0, 8), (0, 8, 8), (0, 16, 15), (1, 0, 16), (1, 16, 8), (1, 24, 6)),
+    ((0, 0, 16), (0, 16, 15), (1, 0, 30)),
+)
+LOAD_QUADS = 16
 RUN = 4
+VECTOR_COLUMNS = 80
 
 ROUND = 4
 OUT_BUFS = 6
-LEAD = 0
-
-
-def vector_columns(columns):
-    return columns * 5 // 8 // 8 * 8
-
-
-def token_groups(unit):
-    groups = []
-    for v in range(2):
-        first = 0
-        for quads in GROUPS[unit][v]:
-            groups.append((v, first, quads))
-            first += quads
-        assert first == (TOKENS - 2 * v + 2) // 4
-    return groups
+SUB = 16
 
 
 def tile_attention_pa_t_kernel(tc, y_attn, w_proj_words, w_proj_scales, b_proj, out):
@@ -61,7 +50,7 @@ def tile_attention_pa_t_kernel(tc, y_attn, w_proj_words, w_proj_scales, b_proj, 
 
     with ExitStack() as stack:
         keep = stack.enter_context(tc.tile_pool(name="keep", bufs=1))
-        x_pool = stack.enter_context(tc.tile_pool(name="x", bufs=X_BUFS))
+        x_pool = stack.enter_context(tc.tile_pool(name="x", bufs=1))
         work = stack.enter_context(tc.tile_pool(name="work", bufs=2))
         out_pool = stack.enter_context(tc.tile_pool(name="out", bufs=OUT_BUFS))
         psum_t = stack.enter_context(tc.psum_pool(name="psum_t", bufs=6))
@@ -80,34 +69,36 @@ def tile_attention_pa_t_kernel(tc, y_attn, w_proj_words, w_proj_scales, b_proj, 
         w_scales = keep.tile([P, PASSES, FEATURES], U8, name="w_scales", align_bytes=64)
 
         def load_tokens(unit, v, first, quads):
-            width = UNITS[unit]
-            x = x_pool.tile([P, 2 * QUADS, width], BF16, name="x")
-            for h in range(2):
-                channel = STRAND_CHANNELS * h + sum(UNITS[:unit])
-                for e in range(2):
-                    token = 4 * first + 2 * v + e
-                    nc.sync.dma_start(
-                        out=x[h:P:2, e : 2 * quads : 2, :],
-                        in_=y_attn[:, token : token + 4 * (quads - 1) + 1 : 4, channel : channel + width],
-                    )
+            x = x_pool.tile(
+                [P, 2 * quads, UNIT_CHANNELS],
+                BF16,
+                name="x_%d_%d_%d" % (unit, v, first),
+                offset=2 * UNIT_CHANNELS * (X_ROW[v] + 2 * first),
+                align_bytes=64,
+            )
+            for part in range(0, quads, LOAD_QUADS):
+                count = min(LOAD_QUADS, quads - part)
+                for h in range(2):
+                    channel = STRAND_CHANNELS * h + UNIT_CHANNELS * unit
+                    for e in range(2):
+                        token = 4 * (first + part) + 2 * v + e
+                        nc.sync.dma_start(
+                            out=x[h:P:2, 2 * part + e : 2 * (part + count) : 2, :],
+                            in_=y_attn[:, token : token + 4 * (count - 1) + 1 : 4, channel : channel + UNIT_CHANNELS],
+                        )
             return x
 
-        def sort_pairs(x, unit, v, first, quads, parity):
+        def sort_pairs(copy, x, unit, v, first, quads, parity, columns):
             rows = 2 * quads
-            columns = UNITS[unit] // 2
-            share = vector_columns(columns)
             plane = (v + parity) % 2
             start = 2 * first + parity * (60 + 2 * v)
             dst = planes[unit][:, plane, :].rearrange("p (c r) -> p c r", r=TOKENS)
-            dst = dst[:, :, start : start + rows]
-            src = x[:, 0:rows, :].rearrange("p r (c two) -> p c r two", two=2)[:, :, :, parity]
-            nc.vector.tensor_copy(
-                out=dst[:, 0:share, :].rearrange("p (q i) r -> p q r i", i=RUN),
-                in_=src[:, 0:share, :].rearrange("p (q i) r -> p q r i", i=RUN),
-            )
-            nc.scalar.copy(
-                out=dst[:, share:, :].rearrange("p (q i) r -> p q r i", i=RUN),
-                in_=src[:, share:, :].rearrange("p (q i) r -> p q r i", i=RUN),
+            dst = dst[:, columns[0] : columns[1], start : start + rows]
+            src = x[:].rearrange("p r (c two) -> p c r two", two=2)
+            src = src[:, columns[0] : columns[1], :, parity]
+            copy(
+                out=dst.rearrange("p (q i) r -> p q r i", i=RUN),
+                in_=src.rearrange("p (q i) r -> p q r i", i=RUN),
             )
 
         def transpose_rows(rows):
@@ -173,81 +164,81 @@ def tile_attention_pa_t_kernel(tc, y_attn, w_proj_words, w_proj_scales, b_proj, 
                     in1=bias[:].unsqueeze(1).to_broadcast([P, count, FEATURES]),
                     op=mybir.AluOpType.add,
                 )
-            waiting.append((rows, result))
-            if state["sorted"] // 2 + X_BUFS >= len(tiles_to_load):
-                for stored_rows, stored in waiting:
-                    nc.sync.dma_start(
-                        out=out_rows[:, stored_rows[0] : stored_rows[0] + len(stored_rows), :],
-                        in_=stored[:, 0 : len(stored_rows), :],
-                    )
-                waiting.clear()
+            nc.sync.dma_start(
+                out=out_rows[:, rows[0] : rows[0] + len(rows), :],
+                in_=result[:, 0 : len(rows), :],
+            )
 
         make_identity(nc, ident[:])
         nc.vector.memset(ones[:], 1.0)
         nc.vector.memset(bias_rows[:], 0.0)
         nc.vector.memset(w_scales[:].bitcast(I32), 0)
 
-        tiles_to_load = [(unit,) + group for unit in range(len(UNITS)) for group in token_groups(unit)]
-        loaded = [load_tokens(*tiles_to_load[t]) for t in range(X_BUFS)]
+        loaded = [load_tokens(0, *load) for load in LOADS[0]]
 
-        def load_weights():
-            nc.sync.dma_start(out=w_words[:].bitcast(I32), in_=w_proj_words.rearrange("g p n -> p g n").bitcast(I32))
-            for quadrant in range(4):
-                nc.sync.dma_start(
-                    out=w_scales[32 * quadrant : 32 * quadrant + 4].bitcast(I32),
-                    in_=w_proj_scales[:, 4 * quadrant : 4 * quadrant + 4, :].rearrange("g r n -> r g n").bitcast(I32),
-                )
-            nc.sync.dma_start(out=bias_rows[0:1, :], in_=b_proj.rearrange("(o n) -> o n", o=1))
+        nc.sync.dma_start(out=w_words[:].bitcast(I32), in_=w_proj_words.rearrange("g p n -> p g n").bitcast(I32))
+        for quadrant in range(4):
+            nc.sync.dma_start(
+                out=w_scales[32 * quadrant : 32 * quadrant + 4].bitcast(I32),
+                in_=w_proj_scales[:, 4 * quadrant : 4 * quadrant + 4, :].rearrange("g r n -> r g n").bitcast(I32),
+            )
+        nc.sync.dma_start(out=bias_rows[0:1, :], in_=b_proj.rearrange("(o n) -> o n", o=1))
 
-        rounds = []
-        first_row = 0
-        for unit in range(len(UNITS)):
-            end_row = sum(UNITS[: unit + 1]) // 2 * WORDS_IN_DOUBLE_COLUMN // (PASSES * P)
-            for r in range(first_row, end_row, ROUND):
-                rounds.append((list(range(r, min(r + ROUND, end_row))), 2 * sum(len(token_groups(u)) for u in range(unit + 1))))
-            first_row = end_row
-
-        last_rows, last_need = rounds.pop()
-        rounds.append((last_rows[:2], last_need))
-        rounds.append((last_rows[2:], last_need))
-
-        state = {"sorted": 0}
-        waiting = []
-
-        def sort_next():
-            t, parity = divmod(state["sorted"], 2)
-            if t < len(tiles_to_load):
-                sort_pairs(loaded[t], *tiles_to_load[t], parity)
-                if parity == 1 and t + X_BUFS < len(tiles_to_load):
-                    if t + X_BUFS == len(token_groups(0)):
-                        load_weights()
-                    loaded.append(load_tokens(*tiles_to_load[t + X_BUFS]))
-                state["sorted"] += 1
-
-        while state["sorted"] < rounds[0][1] + LEAD:
-            sort_next()
+        second = []
+        for x, (v, first, quads) in zip(loaded, LOADS[0]):
+            for parity in range(2):
+                sort_pairs(nc.vector.tensor_copy, x, 0, v, first, quads, parity, (0, VECTOR_COLUMNS))
+                sort_pairs(nc.scalar.copy, x, 0, v, first, quads, parity, (VECTOR_COLUMNS, UNIT_COLUMNS))
+            for load in LOADS[1][len(second) :]:
+                if (load[0], load[1] + load[2]) <= (v, first + quads):
+                    second.append((load_tokens(1, *load), load))
 
         spread = psum_o.tile([P, 2, FEATURES], F32, name="acc")
         nc.tensor.matmul(out=spread[:, 0, :], lhsT=ones[:], rhs=bias_rows[:], start=True, stop=True)
         nc.vector.tensor_copy(out=bias[:], in_=spread[:, 0, :])
 
-        ready = quantise_rows(rounds[0][0], transpose_rows(rounds[0][0]))
-        for k in range(len(rounds)):
-            rows = rounds[k][0]
+        rounds = []
+        for width in [2] + [ROUND] * 14 + [2, 1]:
+            start = rounds[-1][-1] + 1 if rounds else 0
+            rounds.append(list(range(start, start + width)))
+        assert rounds[-1][-1] == STRAND_ROWS - 1
+
+        pieces = []
+        for x, load in second[:-1]:
+            for c in range(0, UNIT_COLUMNS, 2 * SUB):
+                for parity in range(2):
+                    pieces.append((x, load, parity, (c, c + 2 * SUB)))
+        early = len(pieces)
+        for c in range(0, UNIT_COLUMNS, SUB):
+            for parity in range(2):
+                pieces.append(second[-1] + (parity, (c, c + SUB)))
+
+        def pieces_needed(rows):
+            words = PASSES * P * (rows[-1] + 1) - UNIT_PASSES * P
+            if words <= 0:
+                return 0
+            columns = -(-words // (TOKENS // 2))
+            return early + 2 * -(-columns // SUB)
+
+        state = {"sorted": 0}
+
+        def sort_up_to(count):
+            while state["sorted"] < min(count, len(pieces)):
+                i = state["sorted"]
+                x, load, parity, columns = pieces[i]
+                copy = nc.scalar.copy if 3 * i % 8 < 3 else nc.vector.tensor_copy
+                sort_pairs(copy, x, 1, *load, parity, columns)
+                state["sorted"] += 1
+
+        STEPS = 12
+        ready = quantise_rows(rounds[0], transpose_rows(rounds[0]))
+        for k, rows in enumerate(rounds):
             following = rounds[k + 1] if k + 1 < len(rounds) else None
-            fresh = following is not None and following[1] > state["sorted"]
-            if fresh:
-                banks = multiply_rows(rows, *ready)
-                while state["sorted"] < following[1]:
-                    sort_next()
-                add_bias_and_store(rows, banks)
-                ready = quantise_rows(following[0], transpose_rows(following[0]))
-            else:
-                if following is not None:
-                    tiles = transpose_rows(following[0])
-                banks = multiply_rows(rows, *ready)
-                for half_sort in range(1):
-                    sort_next()
-                if following is not None:
-                    ready = quantise_rows(following[0], tiles)
-                add_bias_and_store(rows, banks)
+            if following:
+                tiles = transpose_rows(following)
+            banks = multiply_rows(rows, *ready)
+            need = pieces_needed(rounds[k + 2]) if k + 2 < len(rounds) else len(pieces)
+            sort_up_to(max(need, len(pieces) * k // STEPS))
+            if following:
+                ready = quantise_rows(following, tiles)
+            add_bias_and_store(rows, banks)

@@ -39,8 +39,9 @@ LOAD_QUADS = 16
 RUN = 4
 VECTOR_COLUMNS = 80
 
-ROUND = 4
-OUT_BUFS = 6
+ROUND = 2
+LEAD = 2
+OUT_BUFS = 12
 SUB = 16
 
 
@@ -197,11 +198,7 @@ def tile_attention_pa_t_kernel(tc, y_attn, w_proj_words, w_proj_scales, b_proj, 
         nc.tensor.matmul(out=spread[:, 0, :], lhsT=ones[:], rhs=bias_rows[:], start=True, stop=True)
         nc.vector.tensor_copy(out=bias[:], in_=spread[:, 0, :])
 
-        rounds = []
-        for width in [2] + [ROUND] * 14 + [2, 1]:
-            start = rounds[-1][-1] + 1 if rounds else 0
-            rounds.append(list(range(start, start + width)))
-        assert rounds[-1][-1] == STRAND_ROWS - 1
+        rounds = [list(range(r, min(r + ROUND, STRAND_ROWS))) for r in range(0, STRAND_ROWS, ROUND)]
 
         pieces = []
         for x, load in second[:-1]:
@@ -230,15 +227,19 @@ def tile_attention_pa_t_kernel(tc, y_attn, w_proj_words, w_proj_scales, b_proj, 
                 sort_pairs(copy, x, 1, *load, parity, columns)
                 state["sorted"] += 1
 
-        STEPS = 12
-        ready = quantise_rows(rounds[0], transpose_rows(rounds[0]))
+        STEPS = 24
+        tiles = [transpose_rows(rows) for rows in rounds[:LEAD]]
+        ready = quantise_rows(rounds[0], tiles.pop(0))
         for k, rows in enumerate(rounds):
-            following = rounds[k + 1] if k + 1 < len(rounds) else None
-            if following:
-                tiles = transpose_rows(following)
+            if k + LEAD < len(rounds):
+                tiles.append(transpose_rows(rounds[k + LEAD]))
             banks = multiply_rows(rows, *ready)
-            need = pieces_needed(rounds[k + 2]) if k + 2 < len(rounds) else len(pieces)
+            ahead = k + LEAD + 2
+            need = pieces_needed(rounds[ahead]) if ahead < len(rounds) else len(pieces)
             sort_up_to(max(need, len(pieces) * k // STEPS))
-            if following:
-                ready = quantise_rows(following, tiles)
-            add_bias_and_store(rows, banks)
+            if tiles:
+                ready = quantise_rows(rounds[k + 1], tiles.pop(0))
+            if k > 0:
+                add_bias_and_store(rounds[k - 1], previous)
+            previous = banks
+        add_bias_and_store(rounds[-1], previous)

@@ -71,7 +71,7 @@ def tile_attention_pa_t_kernel(tc, y_attn, w_proj_words, w_proj_scales, b_proj, 
 
         def load_tokens(unit, v, first, quads):
             x = x_pool.tile(
-                [P, 2 * quads, UNIT_CHANNELS],
+                [P, 2, quads, UNIT_CHANNELS],
                 BF16,
                 name="x_%d_%d_%d" % (unit, v, first),
                 offset=2 * UNIT_CHANNELS * (X_ROW[v] + 2 * first),
@@ -84,7 +84,7 @@ def tile_attention_pa_t_kernel(tc, y_attn, w_proj_words, w_proj_scales, b_proj, 
                     for e in range(2):
                         token = 4 * (first + part) + 2 * v + e
                         nc.sync.dma_start(
-                            out=x[h:P:2, 2 * part + e : 2 * (part + count) : 2, :],
+                            out=x[h:P:2, e, part : part + count, :],
                             in_=y_attn[:, token : token + 4 * (count - 1) + 1 : 4, channel : channel + UNIT_CHANNELS],
                         )
             return x
@@ -95,11 +95,11 @@ def tile_attention_pa_t_kernel(tc, y_attn, w_proj_words, w_proj_scales, b_proj, 
             start = 2 * first + parity * (60 + 2 * v)
             dst = planes[unit][:, plane, :].rearrange("p (c r) -> p c r", r=TOKENS)
             dst = dst[:, columns[0] : columns[1], start : start + rows]
-            src = x[:].rearrange("p r (c two) -> p c r two", two=2)
-            src = src[:, columns[0] : columns[1], :, parity]
+            src = x[:].rearrange("p e a (c two) -> p c a e two", two=2)
+            src = src[:, columns[0] : columns[1], :, :, parity]
             copy(
-                out=dst.rearrange("p (q i) r -> p q r i", i=RUN),
-                in_=src.rearrange("p (q i) r -> p q r i", i=RUN),
+                out=dst.rearrange("p (q i) (a e) -> p q a e i", i=RUN, e=2),
+                in_=src.rearrange("p (q i) a e -> p q a e i", i=RUN),
             )
 
         def transpose_rows(rows):

@@ -33,15 +33,16 @@ assert UNIT_CHANNELS * TOKENS == UNIT_PASSES * K_PASS
 X_ROW = (0, 62)
 LOADS = (
     ((0, 0, 8), (0, 8, 8), (0, 16, 15), (1, 0, 16), (1, 16, 8), (1, 24, 6)),
-    ((0, 0, 16), (0, 16, 15), (1, 0, 30)),
+    ((0, 0, 16), (0, 16, 15), (1, 0, 16), (1, 16, 14)),
 )
-LOAD_QUADS = 16
 RUN = 4
 VECTOR_COLUMNS = 80
 
 ROUND = 2
 LEAD = 2
 OUT_BUFS = 12
+MARGIN = 2
+FIRST_STEP, LAST_STEP = 2, 13
 SUB = 16
 
 
@@ -77,16 +78,14 @@ def tile_attention_pa_t_kernel(tc, y_attn, w_proj_words, w_proj_scales, b_proj, 
                 offset=2 * UNIT_CHANNELS * (X_ROW[v] + 2 * first),
                 align_bytes=64,
             )
-            for part in range(0, quads, LOAD_QUADS):
-                count = min(LOAD_QUADS, quads - part)
-                for h in range(2):
-                    channel = STRAND_CHANNELS * h + UNIT_CHANNELS * unit
-                    for e in range(2):
-                        token = 4 * (first + part) + 2 * v + e
-                        nc.sync.dma_start(
-                            out=x[h:P:2, e, part : part + count, :],
-                            in_=y_attn[:, token : token + 4 * (count - 1) + 1 : 4, channel : channel + UNIT_CHANNELS],
-                        )
+            for h in range(2):
+                channel = STRAND_CHANNELS * h + UNIT_CHANNELS * unit
+                for e in range(2):
+                    token = 4 * first + 2 * v + e
+                    nc.sync.dma_start(
+                        out=x[h:P:2, e, :, :],
+                        in_=y_attn[:, token : token + 4 * (quads - 1) + 1 : 4, channel : channel + UNIT_CHANNELS],
+                    )
             return x
 
         def sort_pairs(copy, x, unit, v, first, quads, parity, columns):
@@ -206,9 +205,10 @@ def tile_attention_pa_t_kernel(tc, y_attn, w_proj_words, w_proj_scales, b_proj, 
                 for parity in range(2):
                     pieces.append((x, load, parity, (c, c + 2 * SUB)))
         early = len(pieces)
+        x, load = second[-1]
         for c in range(0, UNIT_COLUMNS, SUB):
             for parity in range(2):
-                pieces.append(second[-1] + (parity, (c, c + SUB)))
+                pieces.append((x, load, parity, (c, c + SUB)))
 
         def pieces_needed(rows):
             words = PASSES * P * (rows[-1] + 1) - UNIT_PASSES * P
@@ -221,25 +221,20 @@ def tile_attention_pa_t_kernel(tc, y_attn, w_proj_words, w_proj_scales, b_proj, 
 
         def sort_up_to(count):
             while state["sorted"] < min(count, len(pieces)):
-                i = state["sorted"]
-                x, load, parity, columns = pieces[i]
-                copy = nc.scalar.copy if 3 * i % 8 < 3 else nc.vector.tensor_copy
+                x, load, parity, columns = pieces[state["sorted"]]
+                copy = nc.vector.tensor_copy if state["sorted"] % 3 else nc.scalar.copy
                 sort_pairs(copy, x, 1, *load, parity, columns)
                 state["sorted"] += 1
 
-        STEPS = 24
         tiles = [transpose_rows(rows) for rows in rounds[:LEAD]]
         ready = quantise_rows(rounds[0], tiles.pop(0))
         for k, rows in enumerate(rounds):
             if k + LEAD < len(rounds):
                 tiles.append(transpose_rows(rounds[k + LEAD]))
             banks = multiply_rows(rows, *ready)
-            ahead = k + LEAD + 2
-            need = pieces_needed(rounds[ahead]) if ahead < len(rounds) else len(pieces)
-            sort_up_to(max(need, len(pieces) * k // STEPS))
             if tiles:
                 ready = quantise_rows(rounds[k + 1], tiles.pop(0))
-            if k > 0:
-                add_bias_and_store(rounds[k - 1], previous)
-            previous = banks
-        add_bias_and_store(rounds[-1], previous)
+            ahead = rounds[min(k + LEAD + MARGIN, len(rounds) - 1)]
+            evenly = early * max(0, k - FIRST_STEP) // (LAST_STEP - FIRST_STEP)
+            sort_up_to(max(pieces_needed(ahead), min(evenly, early)))
+            add_bias_and_store(rows, banks)

@@ -39,6 +39,7 @@ RUN = 4
 VECTOR_COLUMNS = 80
 
 ROUND = 2
+FIRST_COLUMNS = 20
 LEAD = 2
 OUT_BUFS = 12
 MARGIN = 2
@@ -174,7 +175,9 @@ def tile_attention_pa_t_kernel(tc, y_attn, w_proj_words, w_proj_scales, b_proj, 
         nc.vector.memset(bias_rows[:], 0.0)
         nc.vector.memset(w_scales[:].bitcast(I32), 0)
 
-        loaded = [load_tokens(0, *load) for load in LOADS[0]]
+        loaded = [load_tokens(0, *LOADS[0][0])]
+        nc.sync.dma_start(out=bias_rows[0:1, :], in_=b_proj.rearrange("(o n) -> o n", o=1))
+        loaded.extend(load_tokens(0, *load) for load in LOADS[0][1:])
 
         nc.sync.dma_start(out=w_words[:].bitcast(I32), in_=w_proj_words.rearrange("g p n -> p g n").bitcast(I32))
         for quadrant in range(4):
@@ -182,20 +185,23 @@ def tile_attention_pa_t_kernel(tc, y_attn, w_proj_words, w_proj_scales, b_proj, 
                 out=w_scales[32 * quadrant : 32 * quadrant + 4].bitcast(I32),
                 in_=w_proj_scales[:, 4 * quadrant : 4 * quadrant + 4, :].rearrange("g r n -> r g n").bitcast(I32),
             )
-        nc.sync.dma_start(out=bias_rows[0:1, :], in_=b_proj.rearrange("(o n) -> o n", o=1))
 
         second = []
-        for x, (v, first, quads) in zip(loaded, LOADS[0]):
-            for parity in range(2):
-                sort_pairs(nc.vector.tensor_copy, x, 0, v, first, quads, parity, (0, VECTOR_COLUMNS))
-                sort_pairs(nc.scalar.copy, x, 0, v, first, quads, parity, (VECTOR_COLUMNS, UNIT_COLUMNS))
+        for n, (x, (v, first, quads)) in enumerate(zip(loaded, LOADS[0])):
+            if n == len(loaded) // 2:
+                spread = psum_o.tile([P, 2, FEATURES], F32, name="acc")
+                nc.tensor.matmul(out=spread[:, 0, :], lhsT=ones[:], rhs=bias_rows[:], start=True, stop=True)
+                nc.vector.tensor_copy(out=bias[:], in_=spread[:, 0, :])
+            if n < len(loaded) - 1:
+                shares = ((nc.vector.tensor_copy, 0, VECTOR_COLUMNS), (nc.scalar.copy, VECTOR_COLUMNS, UNIT_COLUMNS))
+            else:
+                shares = ((nc.vector.tensor_copy, 0, FIRST_COLUMNS), (nc.vector.tensor_copy, FIRST_COLUMNS, UNIT_COLUMNS))
+            for copy, low, high in shares:
+                for parity in range(2):
+                    sort_pairs(copy, x, 0, v, first, quads, parity, (low, high))
             for load in LOADS[1][len(second) :]:
                 if (load[0], load[1] + load[2]) <= (v, first + quads):
                     second.append((load_tokens(1, *load), load))
-
-        spread = psum_o.tile([P, 2, FEATURES], F32, name="acc")
-        nc.tensor.matmul(out=spread[:, 0, :], lhsT=ones[:], rhs=bias_rows[:], start=True, stop=True)
-        nc.vector.tensor_copy(out=bias[:], in_=spread[:, 0, :])
 
         rounds = [list(range(r, min(r + ROUND, STRAND_ROWS))) for r in range(0, STRAND_ROWS, ROUND)]
 

@@ -33,7 +33,7 @@ assert UNIT_CHANNELS * TOKENS == UNIT_PASSES * K_PASS
 X_ROW = (0, 62)
 LOADS = (
     ((0, 0, 8), (0, 8, 8), (0, 16, 15), (1, 0, 16), (1, 16, 8), (1, 24, 6)),
-    ((0, 0, 16), (0, 16, 15), (1, 0, 16), (1, 16, 14)),
+    ((0, 0, 16), (0, 16, 15), (1, 0, 8), (1, 8, 22)),
 )
 RUN = 4
 VECTOR_COLUMNS = 80
@@ -43,7 +43,8 @@ FIRST_COLUMNS = 20
 LEAD = 2
 OUT_BUFS = 12
 MARGIN = 2
-FIRST_STEP, LAST_STEP = 2, 13
+FIRST_STEP, LAST_STEP = 2, 11
+SHARES = (("vector", 32), ("scalar", 16), ("vector", 32), ("scalar", 16), ("vector", 16), ("scalar", 16))
 SUB = 16
 
 
@@ -205,16 +206,21 @@ def tile_attention_pa_t_kernel(tc, y_attn, w_proj_words, w_proj_scales, b_proj, 
 
         rounds = [list(range(r, min(r + ROUND, STRAND_ROWS))) for r in range(0, STRAND_ROWS, ROUND)]
 
+        vector, scalar = nc.vector.tensor_copy, nc.scalar.copy
         pieces = []
         for x, load in second[:-1]:
-            for c in range(0, UNIT_COLUMNS, 2 * SUB):
-                for parity in range(2):
-                    pieces.append((x, load, parity, (c, c + 2 * SUB)))
+            for parity in range(2):
+                low = 0
+                for copy, width in SHARES:
+                    pieces.append((vector if copy == "vector" else scalar, x, load, parity, (low, low + width)))
+                    low += width
+                assert low == UNIT_COLUMNS
         early = len(pieces)
         x, load = second[-1]
         for c in range(0, UNIT_COLUMNS, SUB):
             for parity in range(2):
-                pieces.append((x, load, parity, (c, c + SUB)))
+                copy = scalar if (len(pieces) - early) % 3 == 2 else vector
+                pieces.append((copy, x, load, parity, (c, c + SUB)))
 
         def pieces_needed(rows):
             words = PASSES * P * (rows[-1] + 1) - UNIT_PASSES * P
@@ -227,8 +233,7 @@ def tile_attention_pa_t_kernel(tc, y_attn, w_proj_words, w_proj_scales, b_proj, 
 
         def sort_up_to(count):
             while state["sorted"] < min(count, len(pieces)):
-                x, load, parity, columns = pieces[state["sorted"]]
-                copy = nc.vector.tensor_copy if state["sorted"] % 3 else nc.scalar.copy
+                copy, x, load, parity, columns = pieces[state["sorted"]]
                 sort_pairs(copy, x, 1, *load, parity, columns)
                 state["sorted"] += 1
 

from contextlib import ExitStack

import concourse.mybir as mybir
from concourse.masks import make_identity

BF16 = mybir.dt.bfloat16
F32 = mybir.dt.float32
I32 = mybir.dt.int32
U32 = mybir.dt.uint32
U8 = mybir.dt.uint8
FP8X4 = mybir.dt.float8_e4m3fn_x4
FP4X4 = mybir.dt.float4_e2m1fn_x4

IMAGES, TOKENS, CHANNELS, FEATURES = 64, 122, 1024, 256
FLOPS = 2 * IMAGES * TOKENS * CHANNELS * FEATURES

P = 128
PACK = 4
K_PASS = P * PACK
PASSES = CHANNELS // K_PASS
STRAND_CHANNELS = CHANNELS // 2
STRAND_ROWS = TOKENS // 2
N_TILE = 128

UNITS = (256, 256)
assert sum(UNITS) == STRAND_CHANNELS
UNIT_CHANNELS = UNITS[0]
UNIT_COLUMNS = UNIT_CHANNELS // 2
PLANE = STRAND_CHANNELS // 2 * TOKENS
UNIT_PASSES = UNIT_CHANNELS * TOKENS // K_PASS
assert UNIT_CHANNELS * TOKENS == UNIT_PASSES * K_PASS

X_ROW = (0, 62)
LOADS = (
    ((0, 0, 8), (0, 8, 8), (0, 16, 15), (1, 0, 16), (1, 16, 8), (1, 24, 6)),
    ((0, 0, 16), (0, 16, 15), (1, 0, 8), (1, 8, 22)),
)
RUN = 4
VECTOR_COLUMNS = 80

ROUND = 2
FIRST_COLUMNS = 20
LEAD = 2
OUT_BUFS = 12
MARGIN = 2
FIRST_STEP, LAST_STEP = 2, 11
SHARES = (("vector", 32), ("scalar", 16), ("vector", 32), ("scalar", 16), ("vector", 16), ("scalar", 16))
SUB = 16


def tile_attention_pa_t_kernel(tc, y_attn, w_proj_words, w_proj_scales, b_proj, out):
    nc = tc.nc
    out_rows = out.flatten_outer_dims().rearrange("(s r) o -> s r o", r=STRAND_ROWS)

    with ExitStack() as stack:
        keep = stack.enter_context(tc.tile_pool(name="keep", bufs=1))
        x_pool = stack.enter_context(tc.tile_pool(name="x", bufs=1))
        work = stack.enter_context(tc.tile_pool(name="work", bufs=2))
        out_pool = stack.enter_context(tc.tile_pool(name="out", bufs=OUT_BUFS))
        psum_t = stack.enter_context(tc.psum_pool(name="psum_t", bufs=6))
        psum_o = stack.enter_context(tc.psum_pool(name="psum_o", bufs=2))
        stack.enter_context(tc.manual_schedule())

        planes = [
            keep.tile([P, 2, PLANE // len(UNITS)], BF16, name="planes%d" % unit, align_bytes=64)
            for unit in range(len(UNITS))
        ]
        ident = keep.tile([P, P], F32, name="ident")
        ones = keep.tile([P, P], BF16, name="ones")
        bias_rows = keep.tile([P, FEATURES], BF16, name="bias_rows")
        bias = keep.tile([P, FEATURES], F32, name="bias")
        w_words = keep.tile([P, PASSES, 2 * FEATURES], U8, name="w_words", align_bytes=64)
        w_scales = keep.tile([P, PASSES, FEATURES], U8, name="w_scales", align_bytes=64)

        def load_tokens(unit, v, first, quads):
            x = x_pool.tile(
                [P, 2, quads, UNIT_CHANNELS],
                BF16,
                name="x_%d_%d_%d" % (unit, v, first),
                offset=2 * UNIT_CHANNELS * (X_ROW[v] + 2 * first),
                align_bytes=64,
            )
            for h in range(2):
                channel = STRAND_CHANNELS * h + UNIT_CHANNELS * unit
                for e in range(2):
                    token = 4 * first + 2 * v + e
                    nc.sync.dma_start(
                        out=x[h:P:2, e, :, :],
                        in_=y_attn[:, token : token + 4 * (quads - 1) + 1 : 4, channel : channel + UNIT_CHANNELS],
                    )
            return x

        def sort_pairs(copy, x, unit, v, first, quads, parity, columns):
            rows = 2 * quads
            plane = (v + parity) % 2
            start = 2 * first + parity * (60 + 2 * v)
            dst = planes[unit][:, plane, :].rearrange("p (c r) -> p c r", r=TOKENS)
            dst = dst[:, columns[0] : columns[1], start : start + rows]
            src = x[:].rearrange("p e a (c two) -> p c a e two", two=2)
            src = src[:, columns[0] : columns[1], :, :, parity]
            copy(
                out=dst.rearrange("p (q i) (a e) -> p q a e i", i=RUN, e=2),
                in_=src.rearrange("p (q i) a e -> p q a e i", i=RUN),
            )

        def transpose_rows(rows):
            tiles = []
            for first in range(0, len(rows), 2):
                grouped = work.tile([P, 2, PASSES, P, PACK], BF16, name="grouped", bufs=4, align_bytes=64)
                for r, row in enumerate(rows[first : first + 2]):
                    turned = psum_t.tile([P, PASSES, 2, P], F32, name="turned")
                    for g in range(PASSES):
                        unit, number = divmod(PASSES * row + g, UNIT_PASSES)
                        for half in range(2):
                            pairs = planes[unit][:, half, :].bitcast(F32)
                            nc.tensor.transpose(
                                out=turned[:, g, half, :],
                                in_=pairs[:, P * number : P * (number + 1)],
                                identity=ident[:],
                            )
                    nc.scalar.copy(
                        out=grouped[:, r].bitcast(F32),
                        in_=turned[:].rearrange("p g half s -> p g s half"),
                    )
                tiles.append(grouped)
            return tiles

        def quantise_rows(rows, tiles):
            codes = work.tile([P, ROUND, PASSES, P], U32, name="codes", align_bytes=64)
            scales = work.tile([P, ROUND, PASSES, P], U8, name="scales", align_bytes=64)
            for t, grouped in enumerate(tiles):
                count = len(rows[2 * t : 2 * t + 2])
                nc.vector.quantize_mx(
                    out=codes[:, 2 * t : 2 * t + count].rearrange("p r g s -> p (r g s)").bitcast(FP8X4),
                    scales=scales[:, 2 * t : 2 * t + count].rearrange("p r g s -> p (r g s)"),
                    in_=grouped[:, 0:count].rearrange("p r g s t -> p (r g s t)"),
                )
            return codes, scales

        def multiply_rows(rows, codes, scales):
            banks = []
            for first in range(0, len(rows), 2):
                acc = psum_o.tile([P, 2, FEATURES], F32, name="acc")
                for r in range(len(rows[first : first + 2])):
                    for n in range(0, FEATURES, N_TILE):
                        for g in range(PASSES):
                            nc.tensor.matmul_mx(
                                out=acc[:, r, n : n + N_TILE],
                                lhsT=codes[:, first + r, g, :].bitcast(FP8X4),
                                lhsT_scale=scales[:, first + r, g, :],
                                rhs=w_words[:, g, 2 * n : 2 * (n + N_TILE)].bitcast(FP4X4),
                                rhs_scale=w_scales[:, g, n : n + N_TILE],
                                start=(g == 0),
                                stop=(g == PASSES - 1),
                            )
                banks.append(acc)
            return banks

        def add_bias_and_store(rows, banks):
            result = out_pool.tile([P, ROUND, FEATURES], F32, name="result")
            for t, acc in enumerate(banks):
                count = len(rows[2 * t : 2 * t + 2])
                nc.vector.tensor_tensor(
                    out=result[:, 2 * t : 2 * t + count, :],
                    in0=acc[:, 0:count, :],
                    in1=bias[:].unsqueeze(1).to_broadcast([P, count, FEATURES]),
                    op=mybir.AluOpType.add,
                )
            nc.sync.dma_start(
                out=out_rows[:, rows[0] : rows[0] + len(rows), :],
                in_=result[:, 0 : len(rows), :],
            )

        make_identity(nc, ident[:])
        nc.vector.memset(ones[:], 1.0)
        nc.vector.memset(bias_rows[:], 0.0)
        nc.vector.memset(w_scales[:].bitcast(I32), 0)

        loaded = [load_tokens(0, *LOADS[0][0])]
        nc.sync.dma_start(out=bias_rows[0:1, :], in_=b_proj.rearrange("(o n) -> o n", o=1))
        loaded.extend(load_tokens(0, *load) for load in LOADS[0][1:])

        nc.sync.dma_start(out=w_words[:].bitcast(I32), in_=w_proj_words.rearrange("g p n -> p g n").bitcast(I32))
        for quadrant in range(4):
            nc.sync.dma_start(
                out=w_scales[32 * quadrant : 32 * quadrant + 4].bitcast(I32),
                in_=w_proj_scales[:, 4 * quadrant : 4 * quadrant + 4, :].rearrange("g r n -> r g n").bitcast(I32),
            )

        second = []
        for n, (x, (v, first, quads)) in enumerate(zip(loaded, LOADS[0])):
            if n == len(loaded) // 2:
                spread = psum_o.tile([P, 2, FEATURES], F32, name="acc")
                nc.tensor.matmul(out=spread[:, 0, :], lhsT=ones[:], rhs=bias_rows[:], start=True, stop=True)
                nc.vector.tensor_copy(out=bias[:], in_=spread[:, 0, :])
            if n < len(loaded) - 1:
                shares = ((nc.vector.tensor_copy, 0, VECTOR_COLUMNS), (nc.scalar.copy, VECTOR_COLUMNS, UNIT_COLUMNS))
            else:
                shares = ((nc.vector.tensor_copy, 0, FIRST_COLUMNS), (nc.vector.tensor_copy, FIRST_COLUMNS, UNIT_COLUMNS))
            for copy, low, high in shares:
                for parity in range(2):
                    sort_pairs(copy, x, 0, v, first, quads, parity, (low, high))
            for load in LOADS[1][len(second) :]:
                if (load[0], load[1] + load[2]) <= (v, first + quads):
                    second.append((load_tokens(1, *load), load))

        rounds = [list(range(r, min(r + ROUND, STRAND_ROWS))) for r in range(0, STRAND_ROWS, ROUND)]

        vector, scalar = nc.vector.tensor_copy, nc.scalar.copy
        pieces = []
        for x, load in second[:-1]:
            for parity in range(2):
                low = 0
                for copy, width in SHARES:
                    pieces.append((vector if copy == "vector" else scalar, x, load, parity, (low, low + width)))
                    low += width
                assert low == UNIT_COLUMNS
        early = len(pieces)
        x, load = second[-1]
        for c in range(0, UNIT_COLUMNS, SUB):
            for parity in range(2):
                copy = scalar if (len(pieces) - early) % 3 == 2 else vector
                pieces.append((copy, x, load, parity, (c, c + SUB)))

        def pieces_needed(rows):
            words = PASSES * P * (rows[-1] + 1) - UNIT_PASSES * P
            if words <= 0:
                return 0
            columns = -(-words // (TOKENS // 2))
            return early + 2 * -(-columns // SUB)

        state = {"sorted": 0}

        def sort_up_to(count):
            while state["sorted"] < min(count, len(pieces)):
                copy, x, load, parity, columns = pieces[state["sorted"]]
                sort_pairs(copy, x, 1, *load, parity, columns)
                state["sorted"] += 1

        tiles = [transpose_rows(rows) for rows in rounds[:LEAD]]
        ready = quantise_rows(rounds[0], tiles.pop(0))
        for k, rows in enumerate(rounds):
            if k + LEAD < len(rounds):
                tiles.append(transpose_rows(rounds[k + LEAD]))
            banks = multiply_rows(rows, *ready)
            if tiles:
                ready = quantise_rows(rounds[k + 1], tiles.pop(0))
            ahead = rounds[min(k + LEAD + MARGIN, len(rounds) - 1)]
            evenly = early * max(0, k - FIRST_STEP) // (LAST_STEP - FIRST_STEP)
            sort_up_to(max(pieces_needed(ahead), min(evenly, early)))
            add_bias_and_store(rows, banks)
